import numpy as np
import ml_dtypes


def mxq(x, axis, fmt="e4m3"):
    dtype, down = {"e4m3": (ml_dtypes.float8_e4m3fn, 7), "e5m2": (ml_dtypes.float8_e5m2, 14)}[fmt]
    v = np.moveaxis(np.asarray(x, np.float32).astype(ml_dtypes.bfloat16).astype(np.float64), axis, -1)
    blocks = v.reshape(v.shape[:-1] + (-1, 32))
    amax = np.abs(blocks).max(-1, keepdims=True)
    byte = np.maximum(np.where(amax > 0, np.frexp(amax)[1] - 1 + 127, 0) - down, 1)
    scale = np.exp2(byte - 127.0)
    codes = (blocks / scale).astype(np.float32).astype(dtype).astype(np.float64)
    return np.moveaxis((codes * scale).reshape(v.shape), -1, axis)


WIDE = False


def mx_kscale(k):
    if not WIDE:
        return np.ones(k)
    levels = np.array([10, -10, 5, -5, 0])
    a = np.random.permutation(np.resize(levels, k // 512 * 4)).reshape(k // 512, 4)
    idx = np.arange(k)
    return np.exp2(a[idx // 512, idx % 128 // 32])


BF16 = ml_dtypes.bfloat16


def bf(x):
    return np.asarray(x, np.float32).astype(BF16)


def f64(x):
    return np.asarray(x).astype(np.float64)


E2M1 = np.array([0.0, 0.5, 1.0, 1.5, 2.0, 3.0, 4.0, 6.0, -0.0, -0.5, -1.0, -1.5, -2.0, -3.0, -4.0, -6.0])


def pack_weight(w, fmt):
    k, n = w.shape
    w = f64(bf(w)).reshape(k // 32, 32, n)
    amax = np.abs(w).max(1)
    if fmt == "e4m3":
        byte = np.frexp(amax)[1] - 1 + 127 - 7
    else:
        mant, ex = np.frexp(amax / 6.0)
        byte = np.where(mant > 0.5, ex, ex - 1) + 127
    byte = np.clip(np.where(amax > 0, byte, 1), 1, 254)
    scaled = (w * np.exp2(127.0 - byte)[:, None, :]).reshape(k, n).astype(np.float32)
    by_word = np.ascontiguousarray(scaled.reshape(k // 512, 128, 4, n).transpose(0, 1, 3, 2))
    if fmt == "e4m3":
        words = by_word.astype(ml_dtypes.float8_e4m3fn).view(np.uint8)
    else:
        c = by_word.astype(ml_dtypes.float4_e2m1fn).view(np.uint8) & 0xF
        words = c[..., 0::2] | (c[..., 1::2] << 4)
    return np.ascontiguousarray(words), np.ascontiguousarray(byte.astype(np.uint8).reshape(k // 512, 16, n))


def unpack_weight(words, scales, fmt):
    g, p, n, _ = words.shape
    if fmt == "e4m3":
        vals = np.ascontiguousarray(words).view(ml_dtypes.float8_e4m3fn).astype(np.float64)
    else:
        nib = np.empty((g, p, n, 4), np.uint8)
        nib[..., 0::2] = words & 0xF
        nib[..., 1::2] = words >> 4
        vals = E2M1[nib]
    vals = vals * np.repeat(np.exp2(scales.astype(np.float64) - 127.0), 8, axis=1)[..., None]
    return vals.transpose(0, 1, 3, 2).reshape(g * 512, n)


B, P0, P1, P2, K0, K1, K2 = 4096, 512, 512, 512, 128, 128, 128
PT = P0 + P1 + P2
KT = K0 + K1 + K2
CLIP0 = 1.0
FMT = "e4m3"


def clip_rows(mat, clip):
    norms = np.sqrt(np.sum(mat * mat, axis=1, keepdims=True))
    scale = np.minimum(clip / norms, 1.0)
    return mat * scale


def setup_inputs():
    s0, s1, s2 = mx_kscale(P0), mx_kscale(P1), mx_kscale(P2)
    r = np.exp2(np.random.uniform(-2.0, 2.0, (B, 1))) / (KT * PT) ** 0.25
    target_grad = bf(np.random.standard_normal((B, PT)) * r * np.concatenate([s0, s1, s2]))
    words0, scales0 = pack_weight(np.random.standard_normal((P0, K0)) / np.sqrt(P0) / s0[:, None], FMT)
    words1, scales1 = pack_weight(np.random.standard_normal((P1, K1)) / np.sqrt(P1) / s1[:, None], FMT)
    words2, scales2 = pack_weight(np.random.standard_normal((P2, K2)) / np.sqrt(P2) / s2[:, None], FMT)
    return {"target_grad": target_grad,
            "bases0_words": words0, "bases0_scales": scales0,
            "bases1_words": words1, "bases1_scales": scales1,
            "bases2_words": words2, "bases2_scales": scales2}


def reference(target_grad, bases0_words, bases0_scales, bases1_words, bases1_scales, bases2_words, bases2_scales):
    g = f64(target_grad)
    embeddings = []
    offset = 0
    for b in (unpack_weight(bases0_words, bases0_scales, FMT),
              unpack_weight(bases1_words, bases1_scales, FMT),
              unpack_weight(bases2_words, bases2_scales, FMT)):
        num_p = b.shape[0]
        embeddings.append(mxq(g[:, offset:offset + num_p], 1, "e4m3") @ b)
        offset += num_p
    embedding = np.concatenate(embeddings, axis=1)
    avg_clipped_embedding = np.sum(clip_rows(embedding, CLIP0), axis=0) / B
    return embedding, avg_clipped_embedding

@@ -1,0 +1,215 @@
+from contextlib import ExitStack
+
+import concourse.mybir as mybir
+from concourse.masks import make_identity
+
+F32 = mybir.dt.float32
+BF16 = mybir.dt.bfloat16
+I32 = mybir.dt.int32
+U32 = mybir.dt.uint32
+U8 = mybir.dt.uint8
+FP8X4 = mybir.dt.float8_e4m3fn_x4
+ALU = mybir.AluOpType
+ACT = mybir.ActivationFunctionType
+
+P = 128
+BATCH = 4096
+GROUPS = 3
+K_PASS = 512
+EMB = 128
+EMB_ALL = GROUPS * EMB
+WORDS = K_PASS // 2
+HALVES = 2
+TILES = 2
+UNITS = BATCH // (P * TILES)
+QUADRANTS = 4
+LIVE = 4
+
+FLOPS = 2 * BATCH * GROUPS * K_PASS * EMB
+
+
+def tile_gep_pa_t_kernel(
+    tc,
+    target_grad,
+    bases0_words,
+    bases0_scales,
+    bases1_words,
+    bases1_scales,
+    bases2_words,
+    bases2_scales,
+    out_0,
+    out_1,
+):
+    nc = tc.nc
+    bases_words = [bases0_words, bases1_words, bases2_words]
+    bases_scales = [bases0_scales, bases1_scales, bases2_scales]
+
+    x_units = target_grad.rearrange("(u p t) k -> u p (t k)", p=P, t=TILES)
+    emb_units = out_0.rearrange("(u p t) j -> u p (t j)", p=P, t=TILES)
+
+    with ExitStack() as ctx:
+        keep = ctx.enter_context(tc.tile_pool(name="keep", bufs=1))
+        x_pool = ctx.enter_context(tc.tile_pool(name="x", bufs=UNITS))
+        emb_pool = ctx.enter_context(tc.tile_pool(name="emb", bufs=UNITS))
+        grouped_pool = ctx.enter_context(tc.tile_pool(name="grouped", bufs=4))
+        mx_pool = ctx.enter_context(tc.tile_pool(name="mx", bufs=4))
+        junk_pool = ctx.enter_context(tc.tile_pool(name="junk", bufs=4))
+        xt_psum = ctx.enter_context(tc.psum_pool(name="xt", bufs=2 * GROUPS))
+        emb_psum = ctx.enter_context(tc.psum_pool(name="embp", bufs=TILES))
+        ctx.enter_context(tc.manual_schedule())
+
+        w_planes = keep.tile([P, GROUPS, EMB], U8, align_bytes=64)
+        nc.vector.memset(w_planes[:].rearrange("p g n -> p (g n)").bitcast(I32), 0)
+        acc = keep.tile([P, TILES, EMB_ALL], F32)
+        nc.vector.memset(acc[:], 0.0)
+        mean_w = keep.tile([P, P], F32)
+        nc.vector.memset(mean_w[:], 1.0 / BATCH)
+        one_col = keep.tile([P, 1], F32)
+        nc.vector.memset(one_col[:], 1.0)
+        ident = keep.tile([P, P], F32)
+        make_identity(nc, ident[:])
+
+        x_sb = []
+
+        def load_x(u):
+            x_tile = x_pool.tile([P, TILES * GROUPS * K_PASS], BF16, name="x_tile")
+            nc.sync.dma_start(out=x_tile[:], in_=x_units[u])
+            x_sb.append(x_tile)
+
+        w_words = keep.tile([P, GROUPS, EMB], U32, align_bytes=64)
+        for g in range(GROUPS):
+            nc.gpsimd.dma_start(
+                out=w_words[:, g, :].bitcast(F32),
+                in_=bases_words[g].rearrange("o p n t -> (o p) (n t)").bitcast(F32),
+            )
+        for half in range(2):
+            load_x(2 * half)
+            load_x(2 * half + 1)
+            for n in range(6 * half, 6 * half + 6):
+                g, q = divmod(n, QUADRANTS)
+                nc.scalar.dma_start(
+                    out=w_planes[32 * q : 32 * q + LIVE, g, :].bitcast(F32),
+                    in_=bases_scales[g][0, LIVE * q : LIVE * (q + 1), :].bitcast(F32),
+                )
+            if half == 0:
+                warm = keep.tile([P, 1], F32)
+                nc.scalar.sqrt(out=warm[:], in_=one_col[:])
+        for u in range(4, UNITS):
+            load_x(u)
+
+        norm2 = keep.tile([P, UNITS * TILES], F32)
+        floored = keep.tile([P, UNITS * TILES], F32)
+        norm = keep.tile([P, UNITS * TILES], F32)
+        clip = keep.tile([P, UNITS * TILES], F32)
+
+        xt_banks = {}
+        grouped = {}
+        codes = {}
+        scales = {}
+        emb_sb = {}
+
+        def transpose(u):
+            x_words = x_sb[u][:].bitcast(F32)
+            for g in range(GROUPS):
+                bank = xt_psum.tile([P, TILES, HALVES, P], F32, name="bank")
+                xt_banks[u, g] = bank
+                for t in range(TILES):
+                    first = (t * GROUPS + g) * WORDS
+                    for h in range(HALVES):
+                        nc.tensor.transpose(
+                            bank[:, t, h, :],
+                            x_words[:, first + h : first + WORDS : HALVES],
+                            ident[:],
+                        )
+
+        def copy_words_out(u):
+            grouped[u] = grouped_pool.tile(
+                [P, GROUPS, TILES * P * 4], BF16, name="grouped_u", align_bytes=64
+            )
+            for g in range(GROUPS):
+                nc.scalar.copy(
+                    out=grouped[u][:, g, :].bitcast(F32).rearrange(
+                        "p (t b h) -> p t b h", t=TILES, h=HALVES
+                    ),
+                    in_=xt_banks[u, g][:].rearrange("p t h b -> p t b h"),
+                )
+
+        def quantise(u):
+            codes[u] = mx_pool.tile([P, GROUPS, TILES * P], U32, name="codes_u", align_bytes=64)
+            scales[u] = mx_pool.tile([P, GROUPS, TILES * P], U8, name="scales_u", align_bytes=64)
+            for g in range(GROUPS):
+                nc.vector.quantize_mx(
+                    out=codes[u][:, g, :].bitcast(FP8X4),
+                    scales=scales[u][:, g, :],
+                    in_=grouped[u][:, g, :],
+                )
+
+        def multiply_and_copy_out(u):
+            emb_sb[u] = emb_pool.tile([P, TILES, EMB_ALL], F32, name="emb_u")
+            for t in range(TILES):
+                emb_bank = emb_psum.tile([P, 512], F32, name="emb_bank")
+                rows = slice(t * P, (t + 1) * P)
+                for g in range(GROUPS):
+                    nc.tensor.matmul_mx(
+                        out=emb_bank[:, g * EMB : (g + 1) * EMB],
+                        lhsT=codes[u][:, g, rows].bitcast(FP8X4),
+                        lhsT_scale=scales[u][:, g, rows],
+                        rhs=w_words[:, g, :].bitcast(FP8X4),
+                        rhs_scale=w_planes[:, g, :],
+                        start=True,
+                        stop=True,
+                    )
+                nc.vector.tensor_copy(out=emb_sb[u][:, t, :], in_=emb_bank[:, 0:EMB_ALL])
+            nc.sync.dma_start(out=emb_units[u], in_=emb_sb[u][:].rearrange("p t j -> p (t j)"))
+
+        def squares(u):
+            for t in range(TILES):
+                junk = junk_pool.tile([P, EMB_ALL], F32, name="junk")
+                col = u * TILES + t
+                nc.scalar.activation(
+                    out=junk[:], in_=emb_sb[u][:, t, :], func=ACT.Square,
+                    accum_out=norm2[:, col : col + 1],
+                )
+
+        def cols(u):
+            return slice(u * TILES, (u + 1) * TILES)
+
+        def weighted_sum(u):
+            for t in range(TILES):
+                col = u * TILES + t
+                nc.vector.scalar_tensor_tensor(
+                    out=acc[:, t, :], in0=emb_sb[u][:, t, :], scalar=clip[:, col : col + 1],
+                    in1=acc[:, t, :], op0=ALU.mult, op1=ALU.add,
+                )
+
+        def live(u):
+            return 0 <= u < UNITS
+
+        for i in range(UNITS + 6):
+            if live(i):
+                transpose(i)
+                copy_words_out(i)
+            if live(i - 4):
+                nc.vector.tensor_scalar_max(out=floored[:, cols(i - 4)], in0=norm2[:, cols(i - 4)], scalar1=1.0)
+            if live(i - 5):
+                nc.vector.reciprocal(out=clip[:, cols(i - 5)], in_=norm[:, cols(i - 5)])
+            if live(i - 1):
+                quantise(i - 1)
+            if live(i - 5):
+                weighted_sum(i - 5)
+            if live(i - 2):
+                multiply_and_copy_out(i - 2)
+            if live(i - 3):
+                squares(i - 3)
+            if live(i - 4):
+                nc.scalar.sqrt(out=norm[:, cols(i - 4)], in_=floored[:, cols(i - 4)])
+
+        avg_bank = emb_psum.tile([P, 512], F32, name="emb_bank")
+        for t in range(TILES):
+            nc.tensor.matmul(
+                out=avg_bank[:, 0:EMB_ALL], lhsT=mean_w[:], rhs=acc[:, t, :],
+                start=(t == 0), stop=(t == TILES - 1),
+            )
+        avg_sb = keep.tile([P, EMB_ALL], F32)
+        nc.vector.tensor_copy(out=avg_sb[:], in_=avg_bank[:, 0:EMB_ALL])
+        nc.sync.dma_start(out=out_1.rearrange("(o j) -> o j", o=1), in_=avg_sb[0:1, :])

@@ -54,7 +54,8 @@ def tile_gep_pa_t_kernel(
         grouped_pool = ctx.enter_context(tc.tile_pool(name="grouped", bufs=4))
         mx_pool = ctx.enter_context(tc.tile_pool(name="mx", bufs=4))
         junk_pool = ctx.enter_context(tc.tile_pool(name="junk", bufs=4))
-        xt_psum = ctx.enter_context(tc.psum_pool(name="xt", bufs=2 * GROUPS))
+        xt_psum = ctx.enter_context(tc.psum_pool(name="xt", bufs=2 * GROUPS - 1))
+        avg_psum = ctx.enter_context(tc.psum_pool(name="avgp", bufs=1))
         emb_psum = ctx.enter_context(tc.psum_pool(name="embp", bufs=TILES))
         ctx.enter_context(tc.manual_schedule())
 
@@ -63,7 +64,7 @@ def tile_gep_pa_t_kernel(
         acc = keep.tile([P, TILES, EMB_ALL], F32)
         nc.vector.memset(acc[:], 0.0)
         mean_w = keep.tile([P, P], F32)
-        nc.vector.memset(mean_w[:], 1.0 / BATCH)
+        nc.vector.memset(mean_w[:], 1.0)
         one_col = keep.tile([P, 1], F32)
         nc.vector.memset(one_col[:], 1.0)
         ident = keep.tile([P, P], F32)
@@ -174,9 +175,25 @@ def tile_gep_pa_t_kernel(
         def cols(u):
             return slice(u * TILES, (u + 1) * TILES)
 
+        avg_bank = avg_psum.tile([P, 512], F32, name="avg_bank")
+
+        def on_tensor(col):
+            return col % 3 == 0 and col < 30
+
+        def weighted_sum_tensor(u):
+            for t in range(TILES):
+                col = u * TILES + t
+                if on_tensor(col):
+                    nc.tensor.matmul(
+                        out=avg_bank[:, 0:EMB_ALL], lhsT=clip[:, col : col + 1].to_broadcast([P, P]),
+                        rhs=emb_sb[u][:, t, :], start=(col == 0), stop=False,
+                    )
+
         def weighted_sum(u):
             for t in range(TILES):
                 col = u * TILES + t
+                if on_tensor(col):
+                    continue
                 nc.vector.scalar_tensor_tensor(
                     out=acc[:, t, :], in0=emb_sb[u][:, t, :], scalar=clip[:, col : col + 1],
                     in1=acc[:, t, :], op0=ALU.mult, op1=ALU.add,
@@ -199,17 +216,18 @@ def tile_gep_pa_t_kernel(
                 weighted_sum(i - 5)
             if live(i - 2):
                 multiply_and_copy_out(i - 2)
+            if live(i - 6):
+                weighted_sum_tensor(i - 6)
             if live(i - 3):
                 squares(i - 3)
             if live(i - 4):
                 nc.scalar.sqrt(out=norm[:, cols(i - 4)], in_=floored[:, cols(i - 4)])
 
-        avg_bank = emb_psum.tile([P, 512], F32, name="emb_bank")
         for t in range(TILES):
             nc.tensor.matmul(
                 out=avg_bank[:, 0:EMB_ALL], lhsT=mean_w[:], rhs=acc[:, t, :],
-                start=(t == 0), stop=(t == TILES - 1),
+                start=False, stop=(t == TILES - 1),
             )
         avg_sb = keep.tile([P, EMB_ALL], F32)
-        nc.vector.tensor_copy(out=avg_sb[:], in_=avg_bank[:, 0:EMB_ALL])
+        nc.vector.tensor_scalar_mul(out=avg_sb[:], in0=avg_bank[:, 0:EMB_ALL], scalar1=1.0 / BATCH)
         nc.sync.dma_start(out=out_1.rearrange("(o j) -> o j", o=1), in_=avg_sb[0:1, :])

@@ -24,6 +24,7 @@ TILES = 2
 UNITS = BATCH // (P * TILES)
 QUADRANTS = 4
 LIVE = 4
+LATE = 11
 
 FLOPS = 2 * BATCH * GROUPS * K_PASS * EMB
 
@@ -61,7 +62,7 @@ def tile_gep_pa_t_kernel(
 
         w_planes = keep.tile([P, GROUPS, EMB], U8, align_bytes=64)
         nc.vector.memset(w_planes[:].rearrange("p g n -> p (g n)").bitcast(I32), 0)
-        acc = keep.tile([P, TILES, EMB_ALL], F32)
+        acc = keep.tile([P, EMB_ALL], F32)
         nc.vector.memset(acc[:], 0.0)
         mean_w = keep.tile([P, P], F32)
         nc.vector.memset(mean_w[:], 1.0)
@@ -94,12 +95,11 @@ def tile_gep_pa_t_kernel(
                 )
             if half == 0:
                 warm = keep.tile([P, 1], F32)
-                nc.scalar.sqrt(out=warm[:], in_=one_col[:])
+                nc.scalar.activation(out=warm[:], in_=one_col[:], func=ACT.Abs_reciprocal_sqrt)
         for u in range(4, UNITS):
             load_x(u)
 
         norm2 = keep.tile([P, UNITS * TILES], F32)
-        floored = keep.tile([P, UNITS * TILES], F32)
         norm = keep.tile([P, UNITS * TILES], F32)
         clip = keep.tile([P, UNITS * TILES], F32)
 
@@ -123,11 +123,16 @@ def tile_gep_pa_t_kernel(
                             ident[:],
                         )
 
+        def clip_root(u):
+            nc.scalar.activation(out=norm[:, cols(u)], in_=norm2[:, cols(u)], func=ACT.Abs_reciprocal_sqrt)
+
         def copy_words_out(u):
             grouped[u] = grouped_pool.tile(
                 [P, GROUPS, TILES * P * 4], BF16, name="grouped_u", align_bytes=64
             )
             for g in range(GROUPS):
+                if g == 1 and live(u - 4):
+                    clip_root(u - 4)
                 nc.scalar.copy(
                     out=grouped[u][:, g, :].bitcast(F32).rearrange(
                         "p (t b h) -> p t b h", t=TILES, h=HALVES
@@ -138,11 +143,11 @@ def tile_gep_pa_t_kernel(
         def quantise(u):
             codes[u] = mx_pool.tile([P, GROUPS, TILES * P], U32, name="codes_u", align_bytes=64)
             scales[u] = mx_pool.tile([P, GROUPS, TILES * P], U8, name="scales_u", align_bytes=64)
-            for g in range(GROUPS):
+            for first, last in ((0, 2), (2, GROUPS)):
                 nc.vector.quantize_mx(
-                    out=codes[u][:, g, :].bitcast(FP8X4),
-                    scales=scales[u][:, g, :],
-                    in_=grouped[u][:, g, :],
+                    out=codes[u][:, first:last, :].rearrange("p g c -> p (g c)").bitcast(FP8X4),
+                    scales=scales[u][:, first:last, :].rearrange("p g c -> p (g c)"),
+                    in_=grouped[u][:, first:last, :].rearrange("p g c -> p (g c)"),
                 )
 
         def multiply_and_copy_out(u):
@@ -178,7 +183,8 @@ def tile_gep_pa_t_kernel(
         avg_bank = avg_psum.tile([P, 512], F32, name="avg_bank")
 
         def on_tensor(col):
-            return col % 3 == 0 and col < 30
+            u, t = divmod(col, TILES)
+            return t == 0 and u < UNITS - 1 and (u >= LATE or u % 2 == 0)
 
         def weighted_sum_tensor(u):
             for t in range(TILES):
@@ -195,21 +201,19 @@ def tile_gep_pa_t_kernel(
                 if on_tensor(col):
                     continue
                 nc.vector.scalar_tensor_tensor(
-                    out=acc[:, t, :], in0=emb_sb[u][:, t, :], scalar=clip[:, col : col + 1],
-                    in1=acc[:, t, :], op0=ALU.mult, op1=ALU.add,
+                    out=acc[:], in0=emb_sb[u][:, t, :], scalar=clip[:, col : col + 1],
+                    in1=acc[:], op0=ALU.mult, op1=ALU.add,
                 )
 
         def live(u):
             return 0 <= u < UNITS
 
-        for i in range(UNITS + 6):
+        for i in range(UNITS + 7):
             if live(i):
                 transpose(i)
                 copy_words_out(i)
-            if live(i - 4):
-                nc.vector.tensor_scalar_max(out=floored[:, cols(i - 4)], in0=norm2[:, cols(i - 4)], scalar1=1.0)
             if live(i - 5):
-                nc.vector.reciprocal(out=clip[:, cols(i - 5)], in_=norm[:, cols(i - 5)])
+                nc.vector.tensor_scalar_min(out=clip[:, cols(i - 5)], in0=norm[:, cols(i - 5)], scalar1=1.0)
             if live(i - 1):
                 quantise(i - 1)
             if live(i - 5):
@@ -218,16 +222,13 @@ def tile_gep_pa_t_kernel(
                 multiply_and_copy_out(i - 2)
             if live(i - 6):
                 weighted_sum_tensor(i - 6)
+            if not live(i) and live(i - 4):
+                clip_root(i - 4)
             if live(i - 3):
                 squares(i - 3)
-            if live(i - 4):
-                nc.scalar.sqrt(out=norm[:, cols(i - 4)], in_=floored[:, cols(i - 4)])
 
-        for t in range(TILES):
-            nc.tensor.matmul(
-                out=avg_bank[:, 0:EMB_ALL], lhsT=mean_w[:], rhs=acc[:, t, :],
-                start=False, stop=(t == TILES - 1),
-            )
+
+        nc.tensor.matmul(out=avg_bank[:, 0:EMB_ALL], lhsT=mean_w[:], rhs=acc[:], start=False, stop=True)
         avg_sb = keep.tile([P, EMB_ALL], F32)
         nc.vector.tensor_scalar_mul(out=avg_sb[:], in0=avg_bank[:, 0:EMB_ALL], scalar1=1.0 / BATCH)
         nc.sync.dma_start(out=out_1.rearrange("(o j) -> o j", o=1), in_=avg_sb[0:1, :])

@@ -143,12 +143,14 @@ def tile_gep_pa_t_kernel(
         def quantise(u):
             codes[u] = mx_pool.tile([P, GROUPS, TILES * P], U32, name="codes_u", align_bytes=64)
             scales[u] = mx_pool.tile([P, GROUPS, TILES * P], U8, name="scales_u", align_bytes=64)
-            for first, last in ((0, 2), (2, GROUPS)):
+            for part, (first, last) in enumerate(((0, 2), (2, GROUPS))):
                 nc.vector.quantize_mx(
                     out=codes[u][:, first:last, :].rearrange("p g c -> p (g c)").bitcast(FP8X4),
                     scales=scales[u][:, first:last, :].rearrange("p g c -> p (g c)"),
                     in_=grouped[u][:, first:last, :].rearrange("p g c -> p (g c)"),
                 )
+                if live(u - 4):
+                    weighted_sum(u - 4, part)
 
         def multiply_and_copy_out(u):
             emb_sb[u] = emb_pool.tile([P, TILES, EMB_ALL], F32, name="emb_u")
@@ -195,11 +197,9 @@ def tile_gep_pa_t_kernel(
                         rhs=emb_sb[u][:, t, :], start=(col == 0), stop=False,
                     )
 
-        def weighted_sum(u):
-            for t in range(TILES):
-                col = u * TILES + t
-                if on_tensor(col):
-                    continue
+        def weighted_sum(u, t):
+            col = u * TILES + t
+            if not on_tensor(col):
                 nc.vector.scalar_tensor_tensor(
                     out=acc[:], in0=emb_sb[u][:, t, :], scalar=clip[:, col : col + 1],
                     in1=acc[:], op0=ALU.mult, op1=ALU.add,
@@ -216,8 +216,9 @@ def tile_gep_pa_t_kernel(
                 nc.vector.tensor_scalar_min(out=clip[:, cols(i - 5)], in0=norm[:, cols(i - 5)], scalar1=1.0)
             if live(i - 1):
                 quantise(i - 1)
-            if live(i - 5):
-                weighted_sum(i - 5)
+            if live(i - 5) and not live(i - 1):
+                for t in range(TILES):
+                    weighted_sum(i - 5, t)
             if live(i - 2):
                 multiply_and_copy_out(i - 2)
             if live(i - 6):

@@ -89,10 +89,12 @@ def tile_gep_pa_t_kernel(
             load_x(2 * half + 1)
             for n in range(6 * half, 6 * half + 6):
                 g, q = divmod(n, QUADRANTS)
-                nc.scalar.dma_start(
-                    out=w_planes[32 * q : 32 * q + LIVE, g, :].bitcast(F32),
-                    in_=bases_scales[g][0, LIVE * q : LIVE * (q + 1), :].bitcast(F32),
-                )
+                plane_rows = w_planes[32 * q : 32 * q + LIVE, g, :]
+                scale_rows = bases_scales[g][0, LIVE * q : LIVE * (q + 1), :]
+                if half == 0:
+                    nc.scalar.dma_start(out=plane_rows.bitcast(F32), in_=scale_rows.bitcast(F32))
+                else:
+                    nc.sync.dma_start(out=plane_rows.bitcast(I32), in_=scale_rows.bitcast(I32))
             if half == 0:
                 warm = keep.tile([P, 1], F32)
                 nc.scalar.activation(out=warm[:], in_=one_col[:], func=ACT.Abs_reciprocal_sqrt)

@@ -22,9 +22,17 @@ WORDS = K_PASS // 2
 HALVES = 2
 TILES = 2
 UNITS = BATCH // (P * TILES)
+BLOCKS_PER_BANK = 2
+BANKS = TILES * GROUPS // BLOCKS_PER_BANK
+FIRST_CUTS = ((0, 3072),)
+XTU = (14, 15)
+EARLY = 0
+VBANKS = ()
+SEMB = ()
+VSQ = ()
 QUADRANTS = 4
 LIVE = 4
-LATE = 11
+TT = (10, 12, 14, 16, 18, 20, 22, 24, 26, 28, 30)
 
 FLOPS = 2 * BATCH * GROUPS * K_PASS * EMB
 
@@ -73,32 +81,38 @@ def tile_gep_pa_t_kernel(
 
         x_sb = []
 
-        def load_x(u):
+        def load_x(u, queue=nc.sync):
             x_tile = x_pool.tile([P, TILES * GROUPS * K_PASS], BF16, name="x_tile")
-            nc.sync.dma_start(out=x_tile[:], in_=x_units[u])
+            for first, last in FIRST_CUTS if u == 0 else ((0, TILES * GROUPS * K_PASS),):
+                queue.dma_start(out=x_tile[:, first:last], in_=x_units[u][:, first:last])
             x_sb.append(x_tile)
 
         w_words = keep.tile([P, GROUPS, EMB], U32, align_bytes=64)
-        for g in range(GROUPS):
+        def load_words(g):
             nc.gpsimd.dma_start(
                 out=w_words[:, g, :].bitcast(F32),
                 in_=bases_words[g].rearrange("o p n t -> (o p) (n t)").bitcast(F32),
             )
-        for half in range(2):
-            load_x(2 * half)
-            load_x(2 * half + 1)
-            for n in range(6 * half, 6 * half + 6):
+
+        def load_scales(first, last, queue, view):
+            for n in range(first, last):
                 g, q = divmod(n, QUADRANTS)
-                plane_rows = w_planes[32 * q : 32 * q + LIVE, g, :]
-                scale_rows = bases_scales[g][0, LIVE * q : LIVE * (q + 1), :]
-                if half == 0:
-                    nc.scalar.dma_start(out=plane_rows.bitcast(F32), in_=scale_rows.bitcast(F32))
-                else:
-                    nc.sync.dma_start(out=plane_rows.bitcast(I32), in_=scale_rows.bitcast(I32))
-            if half == 0:
-                warm = keep.tile([P, 1], F32)
-                nc.scalar.activation(out=warm[:], in_=one_col[:], func=ACT.Abs_reciprocal_sqrt)
-        for u in range(4, UNITS):
+                queue.dma_start(
+                    out=w_planes[32 * q : 32 * q + LIVE, g, :].bitcast(view),
+                    in_=bases_scales[g][0, LIVE * q : LIVE * (q + 1), :].bitcast(view),
+                )
+
+        for g in range(GROUPS):
+            load_words(g)
+        load_x(0)
+        load_scales(4, 6, nc.sync, I32)
+        load_x(1)
+        load_scales(0, 4, nc.scalar, F32)
+        warm = keep.tile([P, 1], F32)
+        nc.scalar.activation(out=warm[:], in_=one_col[:], func=ACT.Abs_reciprocal_sqrt)
+        load_x(2)
+        load_scales(6, 12, nc.sync, I32)
+        for u in range(3, UNITS):
             load_x(u)
 
         norm2 = keep.tile([P, UNITS * TILES], F32)
@@ -113,14 +127,14 @@ def tile_gep_pa_t_kernel(
 
         def transpose(u):
             x_words = x_sb[u][:].bitcast(F32)
-            for g in range(GROUPS):
-                bank = xt_psum.tile([P, TILES, HALVES, P], F32, name="bank")
-                xt_banks[u, g] = bank
-                for t in range(TILES):
-                    first = (t * GROUPS + g) * WORDS
+            for b in range(BANKS):
+                bank = xt_psum.tile([P, BLOCKS_PER_BANK, HALVES, P], F32, name="bank")
+                xt_banks[u, b] = bank
+                for j in range(BLOCKS_PER_BANK):
+                    first = (b * BLOCKS_PER_BANK + j) * WORDS
                     for h in range(HALVES):
                         nc.tensor.transpose(
-                            bank[:, t, h, :],
+                            bank[:, j, h, :],
                             x_words[:, first + h : first + WORDS : HALVES],
                             ident[:],
                         )
@@ -128,54 +142,73 @@ def tile_gep_pa_t_kernel(
         def clip_root(u):
             nc.scalar.activation(out=norm[:, cols(u)], in_=norm2[:, cols(u)], func=ACT.Abs_reciprocal_sqrt)
 
-        def copy_words_out(u):
+        def new_grouped(u):
             grouped[u] = grouped_pool.tile(
-                [P, GROUPS, TILES * P * 4], BF16, name="grouped_u", align_bytes=64
+                [P, BANKS, BLOCKS_PER_BANK * K_PASS], BF16, name="grouped_u", align_bytes=64
             )
+
+        def copy_bank(u, b):
+            copy = nc.vector.tensor_copy if (u, b) in VBANKS else nc.scalar.copy
+            copy(
+                out=grouped[u][:, b, :].bitcast(F32).rearrange(
+                    "p (j r h) -> p j r h", j=BLOCKS_PER_BANK, h=HALVES
+                ),
+                in_=xt_banks[u, b][:].rearrange("p j h r -> p j r h"),
+            )
+
+        def quantise(u, part):
+            if part == 0:
+                codes[u] = mx_pool.tile([P, BANKS, BLOCKS_PER_BANK * P], U32, name="codes_u", align_bytes=64)
+                scales[u] = mx_pool.tile([P, BANKS, BLOCKS_PER_BANK * P], U8, name="scales_u", align_bytes=64)
+            first, last = ((0, 2), (2, BANKS))[part]
+            nc.vector.quantize_mx(
+                out=codes[u][:, first:last, :].rearrange("p b c -> p (b c)").bitcast(FP8X4),
+                scales=scales[u][:, first:last, :].rearrange("p b c -> p (b c)"),
+                in_=grouped[u][:, first:last, :].rearrange("p b c -> p (b c)"),
+            )
+
+        emb_banks = {}
+
+        def multiply(u, t):
+            if t == 0:
+                emb_sb[u] = emb_pool.tile([P, TILES, EMB_ALL], F32, name="emb_u")
+            code_blocks = codes[u][:].rearrange("p b c -> p (b c)")
+            scale_blocks = scales[u][:].rearrange("p b c -> p (b c)")
+            if u in XTU:
+                tile = xt_psum.tile([P, BLOCKS_PER_BANK, HALVES, P], F32, name="bank")
+                emb_bank = tile[:].rearrange("p j h r -> p (j h r)")
+            else:
+                tile = emb_psum.tile([P, 512], F32, name="emb_bank")
+                emb_bank = tile[:]
+            emb_banks[u, t] = emb_bank
             for g in range(GROUPS):
-                if g == 1 and live(u - 4):
-                    clip_root(u - 4)
-                nc.scalar.copy(
-                    out=grouped[u][:, g, :].bitcast(F32).rearrange(
-                        "p (t b h) -> p t b h", t=TILES, h=HALVES
-                    ),
-                    in_=xt_banks[u, g][:].rearrange("p t h b -> p t b h"),
+                block = slice((t * GROUPS + g) * P, (t * GROUPS + g + 1) * P)
+                nc.tensor.matmul_mx(
+                    out=emb_bank[:, g * EMB : (g + 1) * EMB],
+                    lhsT=code_blocks[:, block].bitcast(FP8X4),
+                    lhsT_scale=scale_blocks[:, block],
+                    rhs=w_words[:, g, :].bitcast(FP8X4),
+                    rhs_scale=w_planes[:, g, :],
+                    start=True,
+                    stop=True,
                 )
 
-        def quantise(u):
-            codes[u] = mx_pool.tile([P, GROUPS, TILES * P], U32, name="codes_u", align_bytes=64)
-            scales[u] = mx_pool.tile([P, GROUPS, TILES * P], U8, name="scales_u", align_bytes=64)
-            for part, (first, last) in enumerate(((0, 2), (2, GROUPS))):
-                nc.vector.quantize_mx(
-                    out=codes[u][:, first:last, :].rearrange("p g c -> p (g c)").bitcast(FP8X4),
-                    scales=scales[u][:, first:last, :].rearrange("p g c -> p (g c)"),
-                    in_=grouped[u][:, first:last, :].rearrange("p g c -> p (g c)"),
-                )
-                if live(u - 4):
-                    weighted_sum(u - 4, part)
+        def copy_out(u, t):
+            copy = nc.scalar.copy if (u, t) in SEMB else nc.vector.tensor_copy
+            copy(out=emb_sb[u][:, t, :], in_=emb_banks[u, t][:, 0:EMB_ALL])
 
-        def multiply_and_copy_out(u):
-            emb_sb[u] = emb_pool.tile([P, TILES, EMB_ALL], F32, name="emb_u")
-            for t in range(TILES):
-                emb_bank = emb_psum.tile([P, 512], F32, name="emb_bank")
-                rows = slice(t * P, (t + 1) * P)
-                for g in range(GROUPS):
-                    nc.tensor.matmul_mx(
-                        out=emb_bank[:, g * EMB : (g + 1) * EMB],
-                        lhsT=codes[u][:, g, rows].bitcast(FP8X4),
-                        lhsT_scale=scales[u][:, g, rows],
-                        rhs=w_words[:, g, :].bitcast(FP8X4),
-                        rhs_scale=w_planes[:, g, :],
-                        start=True,
-                        stop=True,
-                    )
-                nc.vector.tensor_copy(out=emb_sb[u][:, t, :], in_=emb_bank[:, 0:EMB_ALL])
+        def store(u):
             nc.sync.dma_start(out=emb_units[u], in_=emb_sb[u][:].rearrange("p t j -> p (t j)"))
 
-        def squares(u):
-            for t in range(TILES):
-                junk = junk_pool.tile([P, EMB_ALL], F32, name="junk")
-                col = u * TILES + t
+        def square(u, t):
+            junk = junk_pool.tile([P, EMB_ALL], F32, name="junk")
+            col = u * TILES + t
+            if (u, t) in VSQ:
+                nc.vector.scalar_tensor_tensor(
+                    out=junk[:], in0=emb_sb[u][:, t, :], scalar=1.0, in1=emb_sb[u][:, t, :],
+                    op0=ALU.mult, op1=ALU.mult, accum_out=norm2[:, col : col + 1],
+                )
+            else:
                 nc.scalar.activation(
                     out=junk[:], in_=emb_sb[u][:, t, :], func=ACT.Square,
                     accum_out=norm2[:, col : col + 1],
@@ -188,7 +221,7 @@ def tile_gep_pa_t_kernel(
 
         def on_tensor(col):
             u, t = divmod(col, TILES)
-            return t == 0 and u < UNITS - 1 and (u >= LATE or u % 2 == 0)
+            return col in TT
 
         def weighted_sum_tensor(u):
             for t in range(TILES):
@@ -196,7 +229,7 @@ def tile_gep_pa_t_kernel(
                 if on_tensor(col):
                     nc.tensor.matmul(
                         out=avg_bank[:, 0:EMB_ALL], lhsT=clip[:, col : col + 1].to_broadcast([P, P]),
-                        rhs=emb_sb[u][:, t, :], start=(col == 0), stop=False,
+                        rhs=emb_sb[u][:, t, :], start=(col == TT[0]), stop=False,
                     )
 
         def weighted_sum(u, t):
@@ -210,25 +243,95 @@ def tile_gep_pa_t_kernel(
         def live(u):
             return 0 <= u < UNITS
 
-        for i in range(UNITS + 7):
-            if live(i):
-                transpose(i)
-                copy_words_out(i)
-            if live(i - 5):
-                nc.vector.tensor_scalar_min(out=clip[:, cols(i - 5)], in0=norm[:, cols(i - 5)], scalar1=1.0)
+        def clip_min(u):
+            nc.vector.tensor_scalar_min(out=clip[:, cols(u)], in0=norm[:, cols(u)], scalar1=1.0)
+
+        def ready(u, step, lag):
+            return live(u) and step == u + lag - (1 if u < EARLY else 0)
+
+        for i in range(UNITS):
+            transpose(i)
+            new_grouped(i)
+            for b in range(BANKS):
+                if b == 1:
+                    for u in range(i):
+                        if ready(u, i, 4):
+                            clip_root(u)
+                if (i, b) not in VBANKS:
+                    copy_bank(i, b)
+            for u in range(i):
+                if ready(u, i, 5):
+                    clip_min(u)
             if live(i - 1):
-                quantise(i - 1)
-            if live(i - 5) and not live(i - 1):
-                for t in range(TILES):
-                    weighted_sum(i - 5, t)
-            if live(i - 2):
-                multiply_and_copy_out(i - 2)
-            if live(i - 6):
-                weighted_sum_tensor(i - 6)
-            if not live(i) and live(i - 4):
-                clip_root(i - 4)
-            if live(i - 3):
-                squares(i - 3)
+                quantise(i - 1, 0)
+            for u in range(i):
+                if ready(u, i, 5):
+                    weighted_sum(u, 0)
+            if live(i - 1):
+                quantise(i - 1, 1)
+            for u in range(i):
+                if ready(u, i, 5):
+                    weighted_sum(u, 1)
+            for u in range(i):
+                if ready(u, i, 2):
+                    for t in range(TILES):
+                        multiply(u, t)
+                        copy_out(u, t)
+                    store(u)
+            for b in range(BANKS):
+                if (i, b) in VBANKS:
+                    copy_bank(i, b)
+            for u in range(i):
+                if ready(u, i, 6):
+                    weighted_sum_tensor(u)
+            for u in range(i):
+                if ready(u, i, 3):
+                    for t in range(TILES):
+                        square(u, t)
+        a, z = UNITS - 2, UNITS - 1
+        multiply(a, 0)
+        multiply(a, 1)
+        weighted_sum_tensor(z - 5)
+        clip_min(z - 4)
+        quantise(z, 0)
+        weighted_sum(z - 4, 0)
+        weighted_sum(z - 4, 1)
+        quantise(z, 1)
+        multiply(z, 0)
+        multiply(z, 1)
+        weighted_sum_tensor(z - 4)
+        square(z - 2, 0)
+        clip_root(z - 3)
+        square(z - 2, 1)
+        copy_out(a, 0)
+        clip_min(z - 3)
+        copy_out(a, 1)
+        store(a)
+        weighted_sum_tensor(z - 3)
+        weighted_sum(z - 3, 0)
+        weighted_sum(z - 3, 1)
+        copy_out(z, 0)
+        square(a, 0)
+        clip_root(z - 2)
+        clip_min(z - 2)
+        copy_out(z, 1)
+        store(z)
+        weighted_sum_tensor(z - 2)
+        weighted_sum(z - 2, 0)
+        weighted_sum(z - 2, 1)
+        square(a, 1)
+        square(z, 0)
+        clip_root(a)
+        square(z, 1)
+        clip_root(z)
+        clip_min(a)
+        weighted_sum_tensor(a)
+        weighted_sum(a, 0)
+        weighted_sum(a, 1)
+        clip_min(z)
+        weighted_sum_tensor(z)
+        weighted_sum(z, 1)
+        weighted_sum(z, 0)
 
 
         nc.tensor.matmul(out=avg_bank[:, 0:EMB_ALL], lhsT=mean_w[:], rhs=acc[:], start=False, stop=True)

@@ -27,12 +27,12 @@ BANKS = TILES * GROUPS // BLOCKS_PER_BANK
 FIRST_CUTS = ((0, 3072),)
 XTU = (14, 15)
 EARLY = 0
-VBANKS = ()
+VBANKS = ((3,2),(7,2))
 SEMB = ()
 VSQ = ()
 QUADRANTS = 4
 LIVE = 4
-TT = (10, 12, 14, 16, 18, 20, 22, 24, 26, 28, 30)
+TT = (0, 4, 8, 12, 16, 20, 22, 24, 26, 28, 30)
 
 FLOPS = 2 * BATCH * GROUPS * K_PASS * EMB
 

from contextlib import ExitStack

import concourse.mybir as mybir
from concourse.masks import make_identity

F32 = mybir.dt.float32
BF16 = mybir.dt.bfloat16
I32 = mybir.dt.int32
U32 = mybir.dt.uint32
U8 = mybir.dt.uint8
FP8X4 = mybir.dt.float8_e4m3fn_x4
ALU = mybir.AluOpType
ACT = mybir.ActivationFunctionType

P = 128
BATCH = 4096
GROUPS = 3
K_PASS = 512
EMB = 128
EMB_ALL = GROUPS * EMB
WORDS = K_PASS // 2
HALVES = 2
TILES = 2
UNITS = BATCH // (P * TILES)
BLOCKS_PER_BANK = 2
BANKS = TILES * GROUPS // BLOCKS_PER_BANK
FIRST_CUTS = ((0, 3072),)
XTU = (14, 15)
EARLY = 0
VBANKS = ((3,2),(7,2))
SEMB = ()
VSQ = ()
QUADRANTS = 4
LIVE = 4
TT = (0, 4, 8, 12, 16, 20, 22, 24, 26, 28, 30)

FLOPS = 2 * BATCH * GROUPS * K_PASS * EMB


def tile_gep_pa_t_kernel(
    tc,
    target_grad,
    bases0_words,
    bases0_scales,
    bases1_words,
    bases1_scales,
    bases2_words,
    bases2_scales,
    out_0,
    out_1,
):
    nc = tc.nc
    bases_words = [bases0_words, bases1_words, bases2_words]
    bases_scales = [bases0_scales, bases1_scales, bases2_scales]

    x_units = target_grad.rearrange("(u p t) k -> u p (t k)", p=P, t=TILES)
    emb_units = out_0.rearrange("(u p t) j -> u p (t j)", p=P, t=TILES)

    with ExitStack() as ctx:
        keep = ctx.enter_context(tc.tile_pool(name="keep", bufs=1))
        x_pool = ctx.enter_context(tc.tile_pool(name="x", bufs=UNITS))
        emb_pool = ctx.enter_context(tc.tile_pool(name="emb", bufs=UNITS))
        grouped_pool = ctx.enter_context(tc.tile_pool(name="grouped", bufs=4))
        mx_pool = ctx.enter_context(tc.tile_pool(name="mx", bufs=4))
        junk_pool = ctx.enter_context(tc.tile_pool(name="junk", bufs=4))
        xt_psum = ctx.enter_context(tc.psum_pool(name="xt", bufs=2 * GROUPS - 1))
        avg_psum = ctx.enter_context(tc.psum_pool(name="avgp", bufs=1))
        emb_psum = ctx.enter_context(tc.psum_pool(name="embp", bufs=TILES))
        ctx.enter_context(tc.manual_schedule())

        w_planes = keep.tile([P, GROUPS, EMB], U8, align_bytes=64)
        nc.vector.memset(w_planes[:].rearrange("p g n -> p (g n)").bitcast(I32), 0)
        acc = keep.tile([P, EMB_ALL], F32)
        nc.vector.memset(acc[:], 0.0)
        mean_w = keep.tile([P, P], F32)
        nc.vector.memset(mean_w[:], 1.0)
        one_col = keep.tile([P, 1], F32)
        nc.vector.memset(one_col[:], 1.0)
        ident = keep.tile([P, P], F32)
        make_identity(nc, ident[:])

        x_sb = []

        def load_x(u, queue=nc.sync):
            x_tile = x_pool.tile([P, TILES * GROUPS * K_PASS], BF16, name="x_tile")
            for first, last in FIRST_CUTS if u == 0 else ((0, TILES * GROUPS * K_PASS),):
                queue.dma_start(out=x_tile[:, first:last], in_=x_units[u][:, first:last])
            x_sb.append(x_tile)

        w_words = keep.tile([P, GROUPS, EMB], U32, align_bytes=64)
        def load_words(g):
            nc.gpsimd.dma_start(
                out=w_words[:, g, :].bitcast(F32),
                in_=bases_words[g].rearrange("o p n t -> (o p) (n t)").bitcast(F32),
            )

        def load_scales(first, last, queue, view):
            for n in range(first, last):
                g, q = divmod(n, QUADRANTS)
                queue.dma_start(
                    out=w_planes[32 * q : 32 * q + LIVE, g, :].bitcast(view),
                    in_=bases_scales[g][0, LIVE * q : LIVE * (q + 1), :].bitcast(view),
                )

        for g in range(GROUPS):
            load_words(g)
        load_x(0)
        load_scales(4, 6, nc.sync, I32)
        load_x(1)
        load_scales(0, 4, nc.scalar, F32)
        warm = keep.tile([P, 1], F32)
        nc.scalar.activation(out=warm[:], in_=one_col[:], func=ACT.Abs_reciprocal_sqrt)
        load_x(2)
        load_scales(6, 12, nc.sync, I32)
        for u in range(3, UNITS):
            load_x(u)

        norm2 = keep.tile([P, UNITS * TILES], F32)
        norm = keep.tile([P, UNITS * TILES], F32)
        clip = keep.tile([P, UNITS * TILES], F32)

        xt_banks = {}
        grouped = {}
        codes = {}
        scales = {}
        emb_sb = {}

        def transpose(u):
            x_words = x_sb[u][:].bitcast(F32)
            for b in range(BANKS):
                bank = xt_psum.tile([P, BLOCKS_PER_BANK, HALVES, P], F32, name="bank")
                xt_banks[u, b] = bank
                for j in range(BLOCKS_PER_BANK):
                    first = (b * BLOCKS_PER_BANK + j) * WORDS
                    for h in range(HALVES):
                        nc.tensor.transpose(
                            bank[:, j, h, :],
                            x_words[:, first + h : first + WORDS : HALVES],
                            ident[:],
                        )

        def clip_root(u):
            nc.scalar.activation(out=norm[:, cols(u)], in_=norm2[:, cols(u)], func=ACT.Abs_reciprocal_sqrt)

        def new_grouped(u):
            grouped[u] = grouped_pool.tile(
                [P, BANKS, BLOCKS_PER_BANK * K_PASS], BF16, name="grouped_u", align_bytes=64
            )

        def copy_bank(u, b):
            copy = nc.vector.tensor_copy if (u, b) in VBANKS else nc.scalar.copy
            copy(
                out=grouped[u][:, b, :].bitcast(F32).rearrange(
                    "p (j r h) -> p j r h", j=BLOCKS_PER_BANK, h=HALVES
                ),
                in_=xt_banks[u, b][:].rearrange("p j h r -> p j r h"),
            )

        def quantise(u, part):
            if part == 0:
                codes[u] = mx_pool.tile([P, BANKS, BLOCKS_PER_BANK * P], U32, name="codes_u", align_bytes=64)
                scales[u] = mx_pool.tile([P, BANKS, BLOCKS_PER_BANK * P], U8, name="scales_u", align_bytes=64)
            first, last = ((0, 2), (2, BANKS))[part]
            nc.vector.quantize_mx(
                out=codes[u][:, first:last, :].rearrange("p b c -> p (b c)").bitcast(FP8X4),
                scales=scales[u][:, first:last, :].rearrange("p b c -> p (b c)"),
                in_=grouped[u][:, first:last, :].rearrange("p b c -> p (b c)"),
            )

        emb_banks = {}

        def multiply(u, t):
            if t == 0:
                emb_sb[u] = emb_pool.tile([P, TILES, EMB_ALL], F32, name="emb_u")
            code_blocks = codes[u][:].rearrange("p b c -> p (b c)")
            scale_blocks = scales[u][:].rearrange("p b c -> p (b c)")
            if u in XTU:
                tile = xt_psum.tile([P, BLOCKS_PER_BANK, HALVES, P], F32, name="bank")
                emb_bank = tile[:].rearrange("p j h r -> p (j h r)")
            else:
                tile = emb_psum.tile([P, 512], F32, name="emb_bank")
                emb_bank = tile[:]
            emb_banks[u, t] = emb_bank
            for g in range(GROUPS):
                block = slice((t * GROUPS + g) * P, (t * GROUPS + g + 1) * P)
                nc.tensor.matmul_mx(
                    out=emb_bank[:, g * EMB : (g + 1) * EMB],
                    lhsT=code_blocks[:, block].bitcast(FP8X4),
                    lhsT_scale=scale_blocks[:, block],
                    rhs=w_words[:, g, :].bitcast(FP8X4),
                    rhs_scale=w_planes[:, g, :],
                    start=True,
                    stop=True,
                )

        def copy_out(u, t):
            copy = nc.scalar.copy if (u, t) in SEMB else nc.vector.tensor_copy
            copy(out=emb_sb[u][:, t, :], in_=emb_banks[u, t][:, 0:EMB_ALL])

        def store(u):
            nc.sync.dma_start(out=emb_units[u], in_=emb_sb[u][:].rearrange("p t j -> p (t j)"))

        def square(u, t):
            junk = junk_pool.tile([P, EMB_ALL], F32, name="junk")
            col = u * TILES + t
            if (u, t) in VSQ:
                nc.vector.scalar_tensor_tensor(
                    out=junk[:], in0=emb_sb[u][:, t, :], scalar=1.0, in1=emb_sb[u][:, t, :],
                    op0=ALU.mult, op1=ALU.mult, accum_out=norm2[:, col : col + 1],
                )
            else:
                nc.scalar.activation(
                    out=junk[:], in_=emb_sb[u][:, t, :], func=ACT.Square,
                    accum_out=norm2[:, col : col + 1],
                )

        def cols(u):
            return slice(u * TILES, (u + 1) * TILES)

        avg_bank = avg_psum.tile([P, 512], F32, name="avg_bank")

        def on_tensor(col):
            u, t = divmod(col, TILES)
            return col in TT

        def weighted_sum_tensor(u):
            for t in range(TILES):
                col = u * TILES + t
                if on_tensor(col):
                    nc.tensor.matmul(
                        out=avg_bank[:, 0:EMB_ALL], lhsT=clip[:, col : col + 1].to_broadcast([P, P]),
                        rhs=emb_sb[u][:, t, :], start=(col == TT[0]), stop=False,
                    )

        def weighted_sum(u, t):
            col = u * TILES + t
            if not on_tensor(col):
                nc.vector.scalar_tensor_tensor(
                    out=acc[:], in0=emb_sb[u][:, t, :], scalar=clip[:, col : col + 1],
                    in1=acc[:], op0=ALU.mult, op1=ALU.add,
                )

        def live(u):
            return 0 <= u < UNITS

        def clip_min(u):
            nc.vector.tensor_scalar_min(out=clip[:, cols(u)], in0=norm[:, cols(u)], scalar1=1.0)

        def ready(u, step, lag):
            return live(u) and step == u + lag - (1 if u < EARLY else 0)

        for i in range(UNITS):
            transpose(i)
            new_grouped(i)
            for b in range(BANKS):
                if b == 1:
                    for u in range(i):
                        if ready(u, i, 4):
                            clip_root(u)
                if (i, b) not in VBANKS:
                    copy_bank(i, b)
            for u in range(i):
                if ready(u, i, 5):
                    clip_min(u)
            if live(i - 1):
                quantise(i - 1, 0)
            for u in range(i):
                if ready(u, i, 5):
                    weighted_sum(u, 0)
            if live(i - 1):
                quantise(i - 1, 1)
            for u in range(i):
                if ready(u, i, 5):
                    weighted_sum(u, 1)
            for u in range(i):
                if ready(u, i, 2):
                    for t in range(TILES):
                        multiply(u, t)
                        copy_out(u, t)
                    store(u)
            for b in range(BANKS):
                if (i, b) in VBANKS:
                    copy_bank(i, b)
            for u in range(i):
                if ready(u, i, 6):
                    weighted_sum_tensor(u)
            for u in range(i):
                if ready(u, i, 3):
                    for t in range(TILES):
                        square(u, t)
        a, z = UNITS - 2, UNITS - 1
        multiply(a, 0)
        multiply(a, 1)
        weighted_sum_tensor(z - 5)
        clip_min(z - 4)
        quantise(z, 0)
        weighted_sum(z - 4, 0)
        weighted_sum(z - 4, 1)
        quantise(z, 1)
        multiply(z, 0)
        multiply(z, 1)
        weighted_sum_tensor(z - 4)
        square(z - 2, 0)
        clip_root(z - 3)
        square(z - 2, 1)
        copy_out(a, 0)
        clip_min(z - 3)
        copy_out(a, 1)
        store(a)
        weighted_sum_tensor(z - 3)
        weighted_sum(z - 3, 0)
        weighted_sum(z - 3, 1)
        copy_out(z, 0)
        square(a, 0)
        clip_root(z - 2)
        clip_min(z - 2)
        copy_out(z, 1)
        store(z)
        weighted_sum_tensor(z - 2)
        weighted_sum(z - 2, 0)
        weighted_sum(z - 2, 1)
        square(a, 1)
        square(z, 0)
        clip_root(a)
        square(z, 1)
        clip_root(z)
        clip_min(a)
        weighted_sum_tensor(a)
        weighted_sum(a, 0)
        weighted_sum(a, 1)
        clip_min(z)
        weighted_sum_tensor(z)
        weighted_sum(z, 1)
        weighted_sum(z, 0)


        nc.tensor.matmul(out=avg_bank[:, 0:EMB_ALL], lhsT=mean_w[:], rhs=acc[:], start=False, stop=True)
        avg_sb = keep.tile([P, EMB_ALL], F32)
        nc.vector.tensor_scalar_mul(out=avg_sb[:], in0=avg_bank[:, 0:EMB_ALL], scalar1=1.0 / BATCH)
        nc.sync.dma_start(out=out_1.rearrange("(o j) -> o j", o=1), in_=avg_sb[0:1, :])
